import numpy as np
import ml_dtypes


def mxq(x, axis, fmt="e4m3"):
    dtype, down = {"e4m3": (ml_dtypes.float8_e4m3fn, 7), "e5m2": (ml_dtypes.float8_e5m2, 14)}[fmt]
    v = np.moveaxis(np.asarray(x, np.float32).astype(ml_dtypes.bfloat16).astype(np.float64), axis, -1)
    blocks = v.reshape(v.shape[:-1] + (-1, 32))
    amax = np.abs(blocks).max(-1, keepdims=True)
    byte = np.maximum(np.where(amax > 0, np.frexp(amax)[1] - 1 + 127, 0) - down, 1)
    scale = np.exp2(byte - 127.0)
    codes = (blocks / scale).astype(np.float32).astype(dtype).astype(np.float64)
    return np.moveaxis((codes * scale).reshape(v.shape), -1, axis)


WIDE = False


def mx_kscale(k):
    if not WIDE:
        return np.ones(k)
    levels = np.array([20, -20, 10, -10, 0])
    a = np.random.permutation(np.resize(levels, k // 512 * 4)).reshape(k // 512, 4)
    idx = np.arange(k)
    return np.exp2(a[idx // 512, idx % 128 // 32])


BF16 = ml_dtypes.bfloat16


def bf(x):
    return np.asarray(x, np.float32).astype(BF16)


def f64(x):
    return np.asarray(x).astype(np.float64)


B, T, S, H, C, CO, W = 2, 128, 8, 8, 1024, 1024, 5
HD = C // H


def setup_inputs():
    u = mx_kscale(CO)
    i = np.arange(T)
    band = np.abs(i[:, None] - i[None, :]) <= W
    e = np.exp(np.random.standard_normal((B, H, S, T, T))) * band
    attn = e / e.sum(-1, keepdims=True)
    v = np.random.standard_normal((B, T, S, H, HD))
    w = np.random.standard_normal((C, CO)) / np.sqrt(C) / u[None, :]
    g = np.random.standard_normal((B, T * S, CO)) * np.exp2(np.random.randint(-12, 1, (B, T * S, 1))) * 16.0 * u
    return {"attn": bf(attn), "v": bf(v), "W_out": bf(w), "grad_out": bf(g)}


def reference(attn, v, W_out, grad_out):
    g = f64(grad_out).reshape(B * T * S, CO)
    gctx = mxq(g, 1, "e5m2") @ mxq(f64(W_out), 1, "e4m3").T
    gctx = gctx.reshape(B, T, S, H, HD).transpose(0, 3, 2, 1, 4)
    gv = f64(attn).transpose(0, 1, 2, 4, 3) @ gctx
    return np.ascontiguousarray(gv.transpose(0, 3, 2, 1, 4))

@@ -1,0 +1,170 @@
+from contextlib import ExitStack
+
+import concourse.mybir as mybir
+from concourse.masks import make_identity
+
+F32 = mybir.dt.float32
+BF16 = mybir.dt.bfloat16
+U32 = mybir.dt.uint32
+U8 = mybir.dt.uint8
+E4M3_X4 = mybir.dt.float8_e4m3fn_x4
+E5M2_X4 = mybir.dt.float8_e5m2_x4
+
+P = 128
+B, T, S, H, HD = 2, 128, 8, 8, 128
+C = H * HD
+CO = 1024
+PACK = 4
+K_PASS = P * PACK
+PASSES = CO // K_PASS
+PLANES = 2
+BANK = 512
+HALVES = C // BANK
+HEADS_PER_BANK = BANK // HD
+UNITS = B * S
+LOAD_AHEAD = 3
+
+FLOPS = 2 * B * T * S * C * CO + 2 * B * H * S * T * T * HD
+BYTES = 2 * (B * H * S * T * T + C * CO + B * T * S * CO) + 4 * B * T * S * C
+
+
+def tile_localtemporalattention_pa_kernel(tc, attn, v, W_out, grad_out, out):
+    nc = tc.nc
+    w_dram = W_out.rearrange("(h p) k -> h p k", p=P)
+    g_dram = grad_out.rearrange("b (t s) k -> b s t k", s=S)
+    attn_dram = attn.rearrange("b h s t u -> b s t h u")
+    out_dram = out.rearrange("b u s h d -> b s u (h d)")
+
+    with ExitStack() as ctx:
+        const = ctx.enter_context(tc.tile_pool(name="const", bufs=1))
+        w_pool = ctx.enter_context(tc.tile_pool(name="w_rows", bufs=H))
+        g_pool = ctx.enter_context(tc.tile_pool(name="g_rows", bufs=LOAD_AHEAD + 2))
+        attn_pool = ctx.enter_context(tc.tile_pool(name="attn_rows", bufs=LOAD_AHEAD + 3))
+        stage = ctx.enter_context(tc.tile_pool(name="stage", bufs=3))
+        result_pool = ctx.enter_context(tc.tile_pool(name="result", bufs=6))
+        psum = ctx.enter_context(tc.psum_pool(name="psum", bufs=8))
+        ctx.enter_context(tc.manual_schedule())
+
+        ident = const.tile([P, P], F32, name="ident")
+        make_identity(nc, ident[:])
+
+        def flip_rows(rows, grouped_words, copy):
+            words = rows[:].bitcast(F32)
+            flipped = psum.tile([P, PASSES, PLANES, P], F32, tag="bank", name="flipped")
+            for c in range(PASSES):
+                for u in range(PLANES):
+                    first = (PLANES * c + u) * P
+                    nc.tensor.transpose(flipped[:, c, u, :], words[:, first : first + P], ident[:])
+            copy(out=grouped_words, in_=flipped[:].rearrange("p c u r -> p c r u"))
+
+        w_rows = []
+        for h in range(H):
+            rows = w_pool.tile([P, CO], BF16, name="w_rows")
+            nc.sync.dma_start(out=rows[:], in_=w_dram[h])
+            w_rows.append(rows)
+
+        g_rows = {}
+        attn_rows = {}
+
+        def load_unit(unit):
+            b, s = divmod(unit, S)
+            g_rows[unit] = g_pool.tile([P, CO], BF16, name="g_rows")
+            nc.sync.dma_start(out=g_rows[unit][:], in_=g_dram[b, s])
+            attn_rows[unit] = attn_pool.tile([P, H * T], BF16, name="attn_rows")
+            nc.sync.dma_start(
+                out=attn_rows[unit][:].rearrange("t (h u) -> t h u", h=H), in_=attn_dram[b, s]
+            )
+
+        for unit in range(LOAD_AHEAD):
+            load_unit(unit)
+
+        w_grouped = const.tile([P, PASSES * C * PACK], BF16, name="w_grouped", align_bytes=64)
+        w_grouped_words = (
+            w_grouped[:].bitcast(F32).rearrange("p (c h r u) -> p c h r u", c=PASSES, h=H, u=PLANES)
+        )
+        w_codes = const.tile([P, PASSES * C], U32, name="w_codes", align_bytes=64)
+        w_scales = const.tile([P, PASSES * C], U8, name="w_scales", align_bytes=64)
+        for h in range(H):
+            copy = nc.vector.tensor_copy if h % 2 == 0 else nc.scalar.copy
+            flip_rows(w_rows[h], w_grouped_words[:, :, h], copy)
+            if h % HEADS_PER_BANK == HEADS_PER_BANK - 1:
+                half = h // HEADS_PER_BANK
+                for c in range(PASSES):
+                    first = c * C + half * BANK
+                    nc.vector.quantize_mx(
+                        out=w_codes[:, first : first + BANK].bitcast(E4M3_X4),
+                        scales=w_scales[:, first : first + BANK],
+                        in_=w_grouped[:, first * PACK : (first + BANK) * PACK],
+                    )
+
+        g_grouped = {}
+        g_codes = {}
+        g_scales = {}
+        attn_f32 = {}
+        gctx = {}
+
+        def flip_unit(unit):
+            g_grouped[unit] = stage.tile([P, PASSES * T * PACK], BF16, name="g_grouped", align_bytes=64)
+            grouped_words = (
+                g_grouped[unit][:].bitcast(F32).rearrange("p (c r u) -> p c r u", c=PASSES, u=PLANES)
+            )
+            flip_rows(g_rows[unit], grouped_words, nc.vector.tensor_copy)
+
+        def widen_unit(unit):
+            attn_f32[unit] = stage.tile([P, H * T], F32, name="attn_f32")
+            nc.vector.tensor_copy(out=attn_f32[unit][:], in_=attn_rows[unit][:])
+
+        def quantise_unit(unit):
+            g_codes[unit] = stage.tile([P, PASSES * T], U32, name="g_codes", align_bytes=64)
+            g_scales[unit] = stage.tile([P, PASSES * T], U8, name="g_scales", align_bytes=64)
+            nc.vector.quantize_mx(
+                out=g_codes[unit][:].bitcast(E5M2_X4), scales=g_scales[unit][:], in_=g_grouped[unit][:]
+            )
+
+        def project_unit(unit):
+            gctx[unit] = stage.tile([P, C], F32, name="gctx")
+            for half in range(HALVES):
+                acc = psum.tile([P, BANK], F32, tag="bank", name="acc")
+                for c in range(PASSES):
+                    first = c * C + half * BANK
+                    nc.tensor.matmul_mx(
+                        out=acc[:],
+                        lhsT=g_codes[unit][:, c * T : (c + 1) * T].bitcast(E5M2_X4),
+                        lhsT_scale=g_scales[unit][:, c * T : (c + 1) * T],
+                        rhs=w_codes[:, first : first + BANK].bitcast(E4M3_X4),
+                        rhs_scale=w_scales[:, first : first + BANK],
+                        start=(c == 0),
+                        stop=(c == PASSES - 1),
+                    )
+                nc.scalar.copy(out=gctx[unit][:, half * BANK : (half + 1) * BANK], in_=acc[:])
+
+        def mix_unit(unit):
+            b, s = divmod(unit, S)
+            for half in range(HALVES):
+                mixed = psum.tile([P, BANK], F32, tag="bank", name="mixed")
+                for j in range(HEADS_PER_BANK):
+                    h = half * HEADS_PER_BANK + j
+                    nc.tensor.matmul(
+                        out=mixed[:, j * HD : (j + 1) * HD],
+                        lhsT=attn_f32[unit][:, h * T : (h + 1) * T],
+                        rhs=gctx[unit][:, h * HD : (h + 1) * HD],
+                        start=True,
+                        stop=True,
+                    )
+                result = result_pool.tile([P, BANK], F32, name="result")
+                nc.scalar.copy(out=result[:], in_=mixed[:])
+                nc.sync.dma_start(out=out_dram[b, s][:, half * BANK : (half + 1) * BANK], in_=result[:])
+
+        for tick in range(UNITS + 2):
+            if tick + LOAD_AHEAD < UNITS:
+                load_unit(tick + LOAD_AHEAD)
+            if tick < UNITS:
+                flip_unit(tick)
+            if 0 <= tick - 1 < UNITS:
+                widen_unit(tick - 1)
+            if tick < UNITS:
+                quantise_unit(tick)
+            if 0 <= tick - 1 < UNITS:
+                project_unit(tick - 1)
+            if 0 <= tick - 2:
+                mix_unit(tick - 2)

@@ -22,6 +22,7 @@ BANK = 512
 HALVES = C // BANK
 HEADS_PER_BANK = BANK // HD
 UNITS = B * S
+HEADS_PER_FLIP = H // (PASSES * PLANES)
 LOAD_AHEAD = 3
 
 FLOPS = 2 * B * T * S * C * CO + 2 * B * H * S * T * T * HD
@@ -103,12 +104,6 @@ def tile_localtemporalattention_pa_kernel(tc, attn, v, W_out, grad_out, out):
         attn_f32 = {}
         gctx = {}
 
-        def flip_unit(unit):
-            g_grouped[unit] = stage.tile([P, PASSES * T * PACK], BF16, name="g_grouped", align_bytes=64)
-            grouped_words = (
-                g_grouped[unit][:].bitcast(F32).rearrange("p (c r u) -> p c r u", c=PASSES, u=PLANES)
-            )
-            flip_rows(g_rows[unit], grouped_words, nc.vector.tensor_copy)
 
         def widen_unit(unit):
             attn_f32[unit] = stage.tile([P, H * T], F32, name="attn_f32")
@@ -138,33 +133,47 @@ def tile_localtemporalattention_pa_kernel(tc, attn, v, W_out, grad_out, out):
                     )
                 nc.scalar.copy(out=gctx[unit][:, half * BANK : (half + 1) * BANK], in_=acc[:])
 
-        def mix_unit(unit):
-            b, s = divmod(unit, S)
+        def mix_and_flip(mix, flip):
+            mixing = 0 <= mix < UNITS
+            flipping = 0 <= flip < UNITS
+            b, s = divmod(mix, S)
+            if flipping:
+                words = g_rows[flip][:].bitcast(F32)
+                flipped = psum.tile([P, PASSES * PLANES, P], F32, tag="bank", name="flipped_g")
             for half in range(HALVES):
-                mixed = psum.tile([P, BANK], F32, tag="bank", name="mixed")
+                if mixing:
+                    mixed = psum.tile([P, BANK], F32, tag="bank", name="mixed")
                 for j in range(HEADS_PER_BANK):
                     h = half * HEADS_PER_BANK + j
-                    nc.tensor.matmul(
-                        out=mixed[:, j * HD : (j + 1) * HD],
-                        lhsT=attn_f32[unit][:, h * T : (h + 1) * T],
-                        rhs=gctx[unit][:, h * HD : (h + 1) * HD],
-                        start=True,
-                        stop=True,
-                    )
-                result = result_pool.tile([P, BANK], F32, name="result")
-                nc.scalar.copy(out=result[:], in_=mixed[:])
-                nc.sync.dma_start(out=out_dram[b, s][:, half * BANK : (half + 1) * BANK], in_=result[:])
+                    if mixing:
+                        nc.tensor.matmul(
+                            out=mixed[:, j * HD : (j + 1) * HD],
+                            lhsT=attn_f32[mix][:, h * T : (h + 1) * T],
+                            rhs=gctx[mix][:, h * HD : (h + 1) * HD],
+                            start=True,
+                            stop=True,
+                        )
+                    if flipping and h % HEADS_PER_FLIP == HEADS_PER_FLIP - 1:
+                        q = h // HEADS_PER_FLIP
+                        nc.tensor.transpose(flipped[:, q, :], words[:, q * P : (q + 1) * P], ident[:])
+                if mixing:
+                    result = result_pool.tile([P, BANK], F32, name="result")
+                    nc.scalar.copy(out=result[:], in_=mixed[:])
+                    nc.sync.dma_start(out=out_dram[b, s][:, half * BANK : (half + 1) * BANK], in_=result[:])
+            if flipping:
+                g_grouped[flip] = stage.tile([P, PASSES * T * PACK], BF16, name="g_grouped", align_bytes=64)
+                nc.vector.tensor_copy(
+                    out=g_grouped[flip][:].bitcast(F32).rearrange("p (c r u) -> p c r u", c=PASSES, u=PLANES),
+                    in_=flipped[:].rearrange("p (c u) r -> p c r u", u=PLANES),
+                )
 
-        for tick in range(UNITS + 2):
+        for tick in range(UNITS + 3):
             if tick + LOAD_AHEAD < UNITS:
                 load_unit(tick + LOAD_AHEAD)
-            if tick < UNITS:
-                flip_unit(tick)
+            if 0 <= tick - 2 < UNITS:
+                widen_unit(tick - 2)
             if 0 <= tick - 1 < UNITS:
-                widen_unit(tick - 1)
-            if tick < UNITS:
-                quantise_unit(tick)
-            if 0 <= tick - 1 < UNITS:
-                project_unit(tick - 1)
-            if 0 <= tick - 2:
-                mix_unit(tick - 2)
+                quantise_unit(tick - 1)
+            if 0 <= tick - 2 < UNITS:
+                project_unit(tick - 2)
+            mix_and_flip(tick - 3, tick)

@@ -20,10 +20,10 @@ PASSES = CO // K_PASS
 PLANES = 2
 BANK = 512
 HALVES = C // BANK
-HEADS_PER_BANK = BANK // HD
+HEADS = BANK // HD
 UNITS = B * S
-HEADS_PER_FLIP = H // (PASSES * PLANES)
-LOAD_AHEAD = 3
+STEPS = HALVES * UNITS
+LOAD_AHEAD = 4
 
 FLOPS = 2 * B * T * S * C * CO + 2 * B * H * S * T * T * HD
 BYTES = 2 * (B * H * S * T * T + C * CO + B * T * S * CO) + 4 * B * T * S * C
@@ -41,6 +41,7 @@ def tile_localtemporalattention_pa_kernel(tc, attn, v, W_out, grad_out, out):
         w_pool = ctx.enter_context(tc.tile_pool(name="w_rows", bufs=H))
         g_pool = ctx.enter_context(tc.tile_pool(name="g_rows", bufs=LOAD_AHEAD + 2))
         attn_pool = ctx.enter_context(tc.tile_pool(name="attn_rows", bufs=LOAD_AHEAD + 3))
+        codes_pool = ctx.enter_context(tc.tile_pool(name="g_codes", bufs=UNITS))
         stage = ctx.enter_context(tc.tile_pool(name="stage", bufs=3))
         result_pool = ctx.enter_context(tc.tile_pool(name="result", bufs=6))
         psum = ctx.enter_context(tc.psum_pool(name="psum", bufs=8))
@@ -48,132 +49,126 @@ def tile_localtemporalattention_pa_kernel(tc, attn, v, W_out, grad_out, out):
 
         ident = const.tile([P, P], F32, name="ident")
         make_identity(nc, ident[:])
-
-        def flip_rows(rows, grouped_words, copy):
-            words = rows[:].bitcast(F32)
-            flipped = psum.tile([P, PASSES, PLANES, P], F32, tag="bank", name="flipped")
-            for c in range(PASSES):
-                for u in range(PLANES):
-                    first = (PLANES * c + u) * P
-                    nc.tensor.transpose(flipped[:, c, u, :], words[:, first : first + P], ident[:])
-            copy(out=grouped_words, in_=flipped[:].rearrange("p c u r -> p c r u"))
-
-        w_rows = []
-        for h in range(H):
-            rows = w_pool.tile([P, CO], BF16, name="w_rows")
-            nc.sync.dma_start(out=rows[:], in_=w_dram[h])
-            w_rows.append(rows)
-
-        g_rows = {}
-        attn_rows = {}
-
-        def load_unit(unit):
-            b, s = divmod(unit, S)
-            g_rows[unit] = g_pool.tile([P, CO], BF16, name="g_rows")
-            nc.sync.dma_start(out=g_rows[unit][:], in_=g_dram[b, s])
-            attn_rows[unit] = attn_pool.tile([P, H * T], BF16, name="attn_rows")
-            nc.sync.dma_start(
-                out=attn_rows[unit][:].rearrange("t (h u) -> t h u", h=H), in_=attn_dram[b, s]
-            )
-
-        for unit in range(LOAD_AHEAD):
-            load_unit(unit)
-
-        w_grouped = const.tile([P, PASSES * C * PACK], BF16, name="w_grouped", align_bytes=64)
-        w_grouped_words = (
-            w_grouped[:].bitcast(F32).rearrange("p (c h r u) -> p c h r u", c=PASSES, h=H, u=PLANES)
-        )
         w_codes = const.tile([P, PASSES * C], U32, name="w_codes", align_bytes=64)
         w_scales = const.tile([P, PASSES * C], U8, name="w_scales", align_bytes=64)
-        for h in range(H):
-            copy = nc.vector.tensor_copy if h % 2 == 0 else nc.scalar.copy
-            flip_rows(w_rows[h], w_grouped_words[:, :, h], copy)
-            if h % HEADS_PER_BANK == HEADS_PER_BANK - 1:
-                half = h // HEADS_PER_BANK
-                for c in range(PASSES):
-                    first = c * C + half * BANK
-                    nc.vector.quantize_mx(
-                        out=w_codes[:, first : first + BANK].bitcast(E4M3_X4),
-                        scales=w_scales[:, first : first + BANK],
-                        in_=w_grouped[:, first * PACK : (first + BANK) * PACK],
-                    )
 
+        w_rows = {}
+        g_rows = {}
+        attn_rows = {}
         g_grouped = {}
         g_codes = {}
         g_scales = {}
         attn_f32 = {}
         gctx = {}
 
+        def load_w_head(h):
+            w_rows[h] = w_pool.tile([P, CO], BF16, name="w_rows")
+            nc.sync.dma_start(out=w_rows[h][:], in_=w_dram[h])
 
-        def widen_unit(unit):
-            attn_f32[unit] = stage.tile([P, H * T], F32, name="attn_f32")
-            nc.vector.tensor_copy(out=attn_f32[unit][:], in_=attn_rows[unit][:])
+        def load_step(step):
+            half, unit = divmod(step, UNITS)
+            b, s = divmod(unit, S)
+            if half == 0:
+                g_rows[unit] = g_pool.tile([P, CO], BF16, name="g_rows")
+                nc.sync.dma_start(out=g_rows[unit][:], in_=g_dram[b, s])
+            attn_rows[step] = attn_pool.tile([P, HEADS * T], BF16, name="attn_rows")
+            nc.sync.dma_start(
+                out=attn_rows[step][:].rearrange("t (h u) -> t h u", h=HEADS),
+                in_=attn_dram[b, s][:, half * HEADS : (half + 1) * HEADS, :],
+            )
+
+        def flip_rows(rows, copy):
+            words = rows[:].bitcast(F32)
+            flipped = psum.tile([P, PASSES, PLANES, P], F32, tag="bank", name="flipped")
+            for c in range(PASSES):
+                for u in range(PLANES):
+                    first = (PLANES * c + u) * P
+                    nc.tensor.transpose(flipped[:, c, u, :], words[:, first : first + P], ident[:])
+            grouped = stage.tile([P, PASSES * P * PACK], BF16, name="grouped", align_bytes=64)
+            copy(
+                out=grouped[:].bitcast(F32).rearrange("p (c r u) -> p c r u", c=PASSES, u=PLANES),
+                in_=flipped[:].rearrange("p c u r -> p c r u"),
+            )
+            return grouped
+
+        def prepare_w_head(h):
+            grouped = flip_rows(w_rows[h], nc.scalar.copy)
+            for c in range(PASSES):
+                first = c * C + h * HD
+                nc.vector.quantize_mx(
+                    out=w_codes[:, first : first + HD].bitcast(E4M3_X4),
+                    scales=w_scales[:, first : first + HD],
+                    in_=grouped[:, c * HD * PACK : (c + 1) * HD * PACK],
+                )
+
+        def flip_unit(unit):
+            g_grouped[unit] = flip_rows(g_rows[unit], nc.vector.tensor_copy)
 
         def quantise_unit(unit):
-            g_codes[unit] = stage.tile([P, PASSES * T], U32, name="g_codes", align_bytes=64)
-            g_scales[unit] = stage.tile([P, PASSES * T], U8, name="g_scales", align_bytes=64)
+            g_codes[unit] = codes_pool.tile([P, PASSES * T], U32, name="g_codes", align_bytes=64)
+            g_scales[unit] = codes_pool.tile([P, PASSES * T], U8, name="g_scales", align_bytes=64)
             nc.vector.quantize_mx(
                 out=g_codes[unit][:].bitcast(E5M2_X4), scales=g_scales[unit][:], in_=g_grouped[unit][:]
             )
 
-        def project_unit(unit):
-            gctx[unit] = stage.tile([P, C], F32, name="gctx")
-            for half in range(HALVES):
-                acc = psum.tile([P, BANK], F32, tag="bank", name="acc")
-                for c in range(PASSES):
-                    first = c * C + half * BANK
-                    nc.tensor.matmul_mx(
-                        out=acc[:],
-                        lhsT=g_codes[unit][:, c * T : (c + 1) * T].bitcast(E5M2_X4),
-                        lhsT_scale=g_scales[unit][:, c * T : (c + 1) * T],
-                        rhs=w_codes[:, first : first + BANK].bitcast(E4M3_X4),
-                        rhs_scale=w_scales[:, first : first + BANK],
-                        start=(c == 0),
-                        stop=(c == PASSES - 1),
-                    )
-                nc.scalar.copy(out=gctx[unit][:, half * BANK : (half + 1) * BANK], in_=acc[:])
+        def widen_step(step):
+            attn_f32[step] = stage.tile([P, HEADS * T], F32, name="attn_f32")
+            nc.vector.tensor_copy(out=attn_f32[step][:], in_=attn_rows[step][:])
 
-        def mix_and_flip(mix, flip):
-            mixing = 0 <= mix < UNITS
-            flipping = 0 <= flip < UNITS
-            b, s = divmod(mix, S)
-            if flipping:
-                words = g_rows[flip][:].bitcast(F32)
-                flipped = psum.tile([P, PASSES * PLANES, P], F32, tag="bank", name="flipped_g")
-            for half in range(HALVES):
-                if mixing:
-                    mixed = psum.tile([P, BANK], F32, tag="bank", name="mixed")
-                for j in range(HEADS_PER_BANK):
-                    h = half * HEADS_PER_BANK + j
-                    if mixing:
-                        nc.tensor.matmul(
-                            out=mixed[:, j * HD : (j + 1) * HD],
-                            lhsT=attn_f32[mix][:, h * T : (h + 1) * T],
-                            rhs=gctx[mix][:, h * HD : (h + 1) * HD],
-                            start=True,
-                            stop=True,
-                        )
-                    if flipping and h % HEADS_PER_FLIP == HEADS_PER_FLIP - 1:
-                        q = h // HEADS_PER_FLIP
-                        nc.tensor.transpose(flipped[:, q, :], words[:, q * P : (q + 1) * P], ident[:])
-                if mixing:
-                    result = result_pool.tile([P, BANK], F32, name="result")
-                    nc.scalar.copy(out=result[:], in_=mixed[:])
-                    nc.sync.dma_start(out=out_dram[b, s][:, half * BANK : (half + 1) * BANK], in_=result[:])
-            if flipping:
-                g_grouped[flip] = stage.tile([P, PASSES * T * PACK], BF16, name="g_grouped", align_bytes=64)
-                nc.vector.tensor_copy(
-                    out=g_grouped[flip][:].bitcast(F32).rearrange("p (c r u) -> p c r u", c=PASSES, u=PLANES),
-                    in_=flipped[:].rearrange("p (c u) r -> p c r u", u=PLANES),
+        def project_step(step):
+            half, unit = divmod(step, UNITS)
+            acc = psum.tile([P, BANK], F32, tag="bank", name="acc")
+            for c in range(PASSES):
+                first = c * C + half * BANK
+                nc.tensor.matmul_mx(
+                    out=acc[:],
+                    lhsT=g_codes[unit][:, c * T : (c + 1) * T].bitcast(E5M2_X4),
+                    lhsT_scale=g_scales[unit][:, c * T : (c + 1) * T],
+                    rhs=w_codes[:, first : first + BANK].bitcast(E4M3_X4),
+                    rhs_scale=w_scales[:, first : first + BANK],
+                    start=(c == 0),
+                    stop=(c == PASSES - 1),
                 )
+            gctx[step] = stage.tile([P, BANK], F32, name="gctx")
+            nc.scalar.copy(out=gctx[step][:], in_=acc[:])
 
-        for tick in range(UNITS + 3):
-            if tick + LOAD_AHEAD < UNITS:
-                load_unit(tick + LOAD_AHEAD)
-            if 0 <= tick - 2 < UNITS:
-                widen_unit(tick - 2)
-            if 0 <= tick - 1 < UNITS:
-                quantise_unit(tick - 1)
-            if 0 <= tick - 2 < UNITS:
-                project_unit(tick - 2)
-            mix_and_flip(tick - 3, tick)
+        def mix_step(step):
+            half, unit = divmod(step, UNITS)
+            b, s = divmod(unit, S)
+            mixed = psum.tile([P, BANK], F32, tag="bank", name="mixed")
+            for j in range(HEADS):
+                nc.tensor.matmul(
+                    out=mixed[:, j * HD : (j + 1) * HD],
+                    lhsT=attn_f32[step][:, j * T : (j + 1) * T],
+                    rhs=gctx[step][:, j * HD : (j + 1) * HD],
+                    start=True,
+                    stop=True,
+                )
+            result = result_pool.tile([P, BANK], F32, name="result")
+            nc.scalar.copy(out=result[:], in_=mixed[:])
+            nc.sync.dma_start(out=out_dram[b, s][:, half * BANK : (half + 1) * BANK], in_=result[:])
+
+        for h in range(HEADS):
+            load_w_head(h)
+        for step in range(LOAD_AHEAD):
+            load_step(step)
+        for h in range(HEADS):
+            prepare_w_head(h)
+
+        for tick in range(STEPS + 2):
+            if tick + LOAD_AHEAD < STEPS:
+                load_step(tick + LOAD_AHEAD)
+            if HEADS + tick < H:
+                load_w_head(HEADS + tick)
+            if tick < UNITS:
+                flip_unit(tick)
+            if HEADS <= HEADS + tick - LOAD_AHEAD < H:
+                prepare_w_head(HEADS + tick - LOAD_AHEAD)
+            if 0 <= tick - 1 < STEPS:
+                widen_step(tick - 1)
+            if tick < UNITS:
+                quantise_unit(tick)
+            if 0 <= tick - 1 < STEPS:
+                project_step(tick - 1)
+            if 0 <= tick - 2:
+                mix_step(tick - 2)

@@ -40,9 +40,9 @@ def tile_localtemporalattention_pa_kernel(tc, attn, v, W_out, grad_out, out):
         const = ctx.enter_context(tc.tile_pool(name="const", bufs=1))
         w_pool = ctx.enter_context(tc.tile_pool(name="w_rows", bufs=H))
         g_pool = ctx.enter_context(tc.tile_pool(name="g_rows", bufs=LOAD_AHEAD + 2))
-        attn_pool = ctx.enter_context(tc.tile_pool(name="attn_rows", bufs=LOAD_AHEAD + 3))
+        attn_pool = ctx.enter_context(tc.tile_pool(name="attn_rows", bufs=LOAD_AHEAD + 5))
         codes_pool = ctx.enter_context(tc.tile_pool(name="g_codes", bufs=UNITS))
-        stage = ctx.enter_context(tc.tile_pool(name="stage", bufs=3))
+        stage = ctx.enter_context(tc.tile_pool(name="stage", bufs=4))
         result_pool = ctx.enter_context(tc.tile_pool(name="result", bufs=6))
         psum = ctx.enter_context(tc.psum_pool(name="psum", bufs=8))
         ctx.enter_context(tc.manual_schedule())
@@ -112,6 +112,8 @@ def tile_localtemporalattention_pa_kernel(tc, attn, v, W_out, grad_out, out):
             )
 
         def widen_step(step):
+            if step % 2 == 1:
+                return
             attn_f32[step] = stage.tile([P, HEADS * T], F32, name="attn_f32")
             nc.vector.tensor_copy(out=attn_f32[step][:], in_=attn_rows[step][:])
 
@@ -129,21 +131,33 @@ def tile_localtemporalattention_pa_kernel(tc, attn, v, W_out, grad_out, out):
                     start=(c == 0),
                     stop=(c == PASSES - 1),
                 )
-            gctx[step] = stage.tile([P, BANK], F32, name="gctx")
-            nc.scalar.copy(out=gctx[step][:], in_=acc[:])
+            if step % 2 == 1:
+                high = stage.tile([P, BANK], BF16, name="gctx_high")
+                nc.scalar.copy(out=high[:], in_=acc[:])
+                low = stage.tile([P, BANK], BF16, name="gctx_low")
+                nc.vector.tensor_sub(out=low[:], in0=acc[:], in1=high[:])
+                gctx[step] = (high, low)
+            else:
+                gctx[step] = stage.tile([P, BANK], F32, name="gctx")
+                nc.scalar.copy(out=gctx[step][:], in_=acc[:])
 
         def mix_step(step):
             half, unit = divmod(step, UNITS)
             b, s = divmod(unit, S)
             mixed = psum.tile([P, BANK], F32, tag="bank", name="mixed")
+            if step % 2 == 1:
+                weights, terms = attn_rows[step], gctx[step]
+            else:
+                weights, terms = attn_f32[step], (gctx[step],)
             for j in range(HEADS):
-                nc.tensor.matmul(
-                    out=mixed[:, j * HD : (j + 1) * HD],
-                    lhsT=attn_f32[step][:, j * T : (j + 1) * T],
-                    rhs=gctx[step][:, j * HD : (j + 1) * HD],
-                    start=True,
-                    stop=True,
-                )
+                for i, term in enumerate(terms):
+                    nc.tensor.matmul(
+                        out=mixed[:, j * HD : (j + 1) * HD],
+                        lhsT=weights[:, j * T : (j + 1) * T],
+                        rhs=term[:, j * HD : (j + 1) * HD],
+                        start=(i == 0),
+                        stop=(i == len(terms) - 1),
+                    )
             result = result_pool.tile([P, BANK], F32, name="result")
             nc.scalar.copy(out=result[:], in_=mixed[:])
             nc.sync.dma_start(out=out_dram[b, s][:, half * BANK : (half + 1) * BANK], in_=result[:])
@@ -155,7 +169,7 @@ def tile_localtemporalattention_pa_kernel(tc, attn, v, W_out, grad_out, out):
         for h in range(HEADS):
             prepare_w_head(h)
 
-        for tick in range(STEPS + 2):
+        for tick in range(STEPS + 3):
             if tick + LOAD_AHEAD < STEPS:
                 load_step(tick + LOAD_AHEAD)
             if HEADS + tick < H:
@@ -170,5 +184,5 @@ def tile_localtemporalattention_pa_kernel(tc, attn, v, W_out, grad_out, out):
                 quantise_unit(tick)
             if 0 <= tick - 1 < STEPS:
                 project_step(tick - 1)
-            if 0 <= tick - 2:
-                mix_step(tick - 2)
+            if 0 <= tick - 3:
+                mix_step(tick - 3)

@@ -22,8 +22,13 @@ BANK = 512
 HALVES = C // BANK
 HEADS = BANK // HD
 UNITS = B * S
-STEPS = HALVES * UNITS
-LOAD_AHEAD = 4
+LEAD = 6
+ORDER = [(unit, half) for half in range(HALVES) for unit in range(LEAD)] + [
+    (unit, half) for unit in range(LEAD, UNITS) for half in range(HALVES)
+]
+STEPS = len(ORDER)
+FIRST = [ORDER.index((unit, 0)) for unit in range(UNITS)]
+LOAD_AHEAD = 6
 
 FLOPS = 2 * B * T * S * C * CO + 2 * B * H * S * T * T * HD
 BYTES = 2 * (B * H * S * T * T + C * CO + B * T * S * CO) + 4 * B * T * S * C
@@ -39,11 +44,11 @@ def tile_localtemporalattention_pa_kernel(tc, attn, v, W_out, grad_out, out):
     with ExitStack() as ctx:
         const = ctx.enter_context(tc.tile_pool(name="const", bufs=1))
         w_pool = ctx.enter_context(tc.tile_pool(name="w_rows", bufs=H))
-        g_pool = ctx.enter_context(tc.tile_pool(name="g_rows", bufs=LOAD_AHEAD + 2))
-        attn_pool = ctx.enter_context(tc.tile_pool(name="attn_rows", bufs=LOAD_AHEAD + 5))
+        g_pool = ctx.enter_context(tc.tile_pool(name="g_rows", bufs=8))
+        attn_pool = ctx.enter_context(tc.tile_pool(name="attn_rows", bufs=LEAD + 5))
         codes_pool = ctx.enter_context(tc.tile_pool(name="g_codes", bufs=UNITS))
-        stage = ctx.enter_context(tc.tile_pool(name="stage", bufs=4))
-        result_pool = ctx.enter_context(tc.tile_pool(name="result", bufs=6))
+        stage = ctx.enter_context(tc.tile_pool(name="stage", bufs=5))
+        result_pool = ctx.enter_context(tc.tile_pool(name="result", bufs=LEAD + 2))
         psum = ctx.enter_context(tc.psum_pool(name="psum", bufs=8))
         ctx.enter_context(tc.manual_schedule())
 
@@ -55,26 +60,25 @@ def tile_localtemporalattention_pa_kernel(tc, attn, v, W_out, grad_out, out):
         w_rows = {}
         g_rows = {}
         attn_rows = {}
+        w_grouped = {}
         g_grouped = {}
         g_codes = {}
         g_scales = {}
         attn_f32 = {}
         gctx = {}
+        results = {}
 
         def load_w_head(h):
             w_rows[h] = w_pool.tile([P, CO], BF16, name="w_rows")
             nc.sync.dma_start(out=w_rows[h][:], in_=w_dram[h])
 
-        def load_step(step):
-            half, unit = divmod(step, UNITS)
+        def load_unit(unit):
             b, s = divmod(unit, S)
-            if half == 0:
-                g_rows[unit] = g_pool.tile([P, CO], BF16, name="g_rows")
-                nc.sync.dma_start(out=g_rows[unit][:], in_=g_dram[b, s])
-            attn_rows[step] = attn_pool.tile([P, HEADS * T], BF16, name="attn_rows")
+            g_rows[unit] = g_pool.tile([P, CO], BF16, name="g_rows")
+            nc.sync.dma_start(out=g_rows[unit][:], in_=g_dram[b, s])
+            attn_rows[unit] = attn_pool.tile([P, H * T], BF16, name="attn_rows")
             nc.sync.dma_start(
-                out=attn_rows[step][:].rearrange("t (h u) -> t h u", h=HEADS),
-                in_=attn_dram[b, s][:, half * HEADS : (half + 1) * HEADS, :],
+                out=attn_rows[unit][:].rearrange("t (h u) -> t h u", h=H), in_=attn_dram[b, s]
             )
 
         def flip_rows(rows, copy):
@@ -91,14 +95,16 @@ def tile_localtemporalattention_pa_kernel(tc, attn, v, W_out, grad_out, out):
             )
             return grouped
 
-        def prepare_w_head(h):
-            grouped = flip_rows(w_rows[h], nc.scalar.copy)
+        def flip_w_head(h, copy):
+            w_grouped[h] = flip_rows(w_rows[h], copy)
+
+        def quantise_w_head(h):
             for c in range(PASSES):
                 first = c * C + h * HD
                 nc.vector.quantize_mx(
                     out=w_codes[:, first : first + HD].bitcast(E4M3_X4),
                     scales=w_scales[:, first : first + HD],
-                    in_=grouped[:, c * HD * PACK : (c + 1) * HD * PACK],
+                    in_=w_grouped[h][:, c * HD * PACK : (c + 1) * HD * PACK],
                 )
 
         def flip_unit(unit):
@@ -111,14 +117,21 @@ def tile_localtemporalattention_pa_kernel(tc, attn, v, W_out, grad_out, out):
                 out=g_codes[unit][:].bitcast(E5M2_X4), scales=g_scales[unit][:], in_=g_grouped[unit][:]
             )
 
+        def is_split(step):
+            return sum(ORDER[step]) % 2 == 1
+
         def widen_step(step):
-            if step % 2 == 1:
+            unit, half = ORDER[step]
+            if is_split(step):
                 return
             attn_f32[step] = stage.tile([P, HEADS * T], F32, name="attn_f32")
-            nc.vector.tensor_copy(out=attn_f32[step][:], in_=attn_rows[step][:])
+            nc.vector.tensor_copy(
+                out=attn_f32[step][:],
+                in_=attn_rows[unit][:, half * HEADS * T : (half + 1) * HEADS * T],
+            )
 
         def project_step(step):
-            half, unit = divmod(step, UNITS)
+            unit, half = ORDER[step]
             acc = psum.tile([P, BANK], F32, tag="bank", name="acc")
             for c in range(PASSES):
                 first = c * C + half * BANK
@@ -131,7 +144,7 @@ def tile_localtemporalattention_pa_kernel(tc, attn, v, W_out, grad_out, out):
                     start=(c == 0),
                     stop=(c == PASSES - 1),
                 )
-            if step % 2 == 1:
+            if is_split(step):
                 high = stage.tile([P, BANK], BF16, name="gctx_high")
                 nc.scalar.copy(out=high[:], in_=acc[:])
                 low = stage.tile([P, BANK], BF16, name="gctx_low")
@@ -142,46 +155,64 @@ def tile_localtemporalattention_pa_kernel(tc, attn, v, W_out, grad_out, out):
                 nc.scalar.copy(out=gctx[step][:], in_=acc[:])
 
         def mix_step(step):
-            half, unit = divmod(step, UNITS)
+            unit, half = ORDER[step]
             b, s = divmod(unit, S)
             mixed = psum.tile([P, BANK], F32, tag="bank", name="mixed")
-            if step % 2 == 1:
-                weights, terms = attn_rows[step], gctx[step]
+            if is_split(step):
+                weights, first, terms = attn_rows[unit], half * HEADS * T, gctx[step]
             else:
-                weights, terms = attn_f32[step], (gctx[step],)
+                weights, first, terms = attn_f32[step], 0, (gctx[step],)
             for j in range(HEADS):
                 for i, term in enumerate(terms):
                     nc.tensor.matmul(
                         out=mixed[:, j * HD : (j + 1) * HD],
-                        lhsT=weights[:, j * T : (j + 1) * T],
+                        lhsT=weights[:, first + j * T : first + (j + 1) * T],
                         rhs=term[:, j * HD : (j + 1) * HD],
                         start=(i == 0),
                         stop=(i == len(terms) - 1),
                     )
-            result = result_pool.tile([P, BANK], F32, name="result")
-            nc.scalar.copy(out=result[:], in_=mixed[:])
-            nc.sync.dma_start(out=out_dram[b, s][:, half * BANK : (half + 1) * BANK], in_=result[:])
+            if half == 0:
+                results[unit] = result_pool.tile([P, C], F32, name="result")
+            columns = slice(half * BANK, (half + 1) * BANK)
+            nc.scalar.copy(out=results[unit][:, columns], in_=mixed[:])
+            if unit == UNITS - 1:
+                nc.sync.dma_start(out=out_dram[b, s][:, columns], in_=results[unit][:, columns])
+            elif half == HALVES - 1:
+                nc.sync.dma_start(out=out_dram[b, s], in_=results[unit][:])
 
-        for h in range(HEADS):
-            load_w_head(h)
-        for step in range(LOAD_AHEAD):
-            load_step(step)
-        for h in range(HEADS):
-            prepare_w_head(h)
+        load_w_head(0)
+        load_w_head(1)
+        load_w_head(2)
+        load_unit(0)
+        load_w_head(3)
+        load_unit(1)
+        for h in range(3):
+            flip_w_head(h, nc.vector.tensor_copy if h == 1 else nc.scalar.copy)
+        quantise_w_head(0)
+        flip_unit(0)
+        flip_w_head(3, nc.scalar.copy)
+        for h in range(1, HEADS):
+            quantise_w_head(h)
+            if h == HEADS - 2:
+                quantise_unit(0)
 
         for tick in range(STEPS + 3):
-            if tick + LOAD_AHEAD < STEPS:
-                load_step(tick + LOAD_AHEAD)
             if HEADS + tick < H:
                 load_w_head(HEADS + tick)
-            if tick < UNITS:
-                flip_unit(tick)
-            if HEADS <= HEADS + tick - LOAD_AHEAD < H:
-                prepare_w_head(HEADS + tick - LOAD_AHEAD)
+            for unit in range(2, UNITS):
+                if tick == max(unit - 2, FIRST[unit] - LOAD_AHEAD):
+                    load_unit(unit)
+            w_head = HEADS + tick - 2
+            if HEADS <= w_head < H:
+                flip_w_head(w_head, nc.scalar.copy)
+            if 0 < tick and tick in FIRST:
+                flip_unit(FIRST.index(tick))
+            if HEADS <= w_head < H:
+                quantise_w_head(w_head)
             if 0 <= tick - 1 < STEPS:
                 widen_step(tick - 1)
-            if tick < UNITS:
-                quantise_unit(tick)
+            if 0 < tick and tick in FIRST:
+                quantise_unit(FIRST.index(tick))
             if 0 <= tick - 1 < STEPS:
                 project_step(tick - 1)
             if 0 <= tick - 3:

@@ -22,13 +22,13 @@ BANK = 512
 HALVES = C // BANK
 HEADS = BANK // HD
 UNITS = B * S
-LEAD = 6
+LEAD = 8
 ORDER = [(unit, half) for half in range(HALVES) for unit in range(LEAD)] + [
     (unit, half) for unit in range(LEAD, UNITS) for half in range(HALVES)
 ]
 STEPS = len(ORDER)
 FIRST = [ORDER.index((unit, 0)) for unit in range(UNITS)]
-LOAD_AHEAD = 6
+FIRST_LOADS, LOADS_PER_TICK = 9, 3
 
 FLOPS = 2 * B * T * S * C * CO + 2 * B * H * S * T * T * HD
 BYTES = 2 * (B * H * S * T * T + C * CO + B * T * S * CO) + 4 * B * T * S * C
@@ -44,8 +44,8 @@ def tile_localtemporalattention_pa_kernel(tc, attn, v, W_out, grad_out, out):
     with ExitStack() as ctx:
         const = ctx.enter_context(tc.tile_pool(name="const", bufs=1))
         w_pool = ctx.enter_context(tc.tile_pool(name="w_rows", bufs=H))
-        g_pool = ctx.enter_context(tc.tile_pool(name="g_rows", bufs=8))
-        attn_pool = ctx.enter_context(tc.tile_pool(name="attn_rows", bufs=LEAD + 5))
+        g_pool = ctx.enter_context(tc.tile_pool(name="g_rows", bufs=UNITS))
+        attn_pool = ctx.enter_context(tc.tile_pool(name="attn_rows", bufs=UNITS))
         codes_pool = ctx.enter_context(tc.tile_pool(name="g_codes", bufs=UNITS))
         stage = ctx.enter_context(tc.tile_pool(name="stage", bufs=5))
         result_pool = ctx.enter_context(tc.tile_pool(name="result", bufs=LEAD + 2))
@@ -72,13 +72,18 @@ def tile_localtemporalattention_pa_kernel(tc, attn, v, W_out, grad_out, out):
             w_rows[h] = w_pool.tile([P, CO], BF16, name="w_rows")
             nc.sync.dma_start(out=w_rows[h][:], in_=w_dram[h])
 
-        def load_unit(unit):
+        def load_g(unit):
             b, s = divmod(unit, S)
             g_rows[unit] = g_pool.tile([P, CO], BF16, name="g_rows")
             nc.sync.dma_start(out=g_rows[unit][:], in_=g_dram[b, s])
-            attn_rows[unit] = attn_pool.tile([P, H * T], BF16, name="attn_rows")
+
+        def load_attn(unit, first, heads):
+            b, s = divmod(unit, S)
+            if first == 0:
+                attn_rows[unit] = attn_pool.tile([P, H * T], BF16, name="attn_rows")
             nc.sync.dma_start(
-                out=attn_rows[unit][:].rearrange("t (h u) -> t h u", h=H), in_=attn_dram[b, s]
+                out=attn_rows[unit][:].rearrange("t (h u) -> t h u", h=H)[:, first : first + heads, :],
+                in_=attn_dram[b, s][:, first : first + heads, :],
             )
 
         def flip_rows(rows, copy):
@@ -180,12 +185,23 @@ def tile_localtemporalattention_pa_kernel(tc, attn, v, W_out, grad_out, out):
             elif half == HALVES - 1:
                 nc.sync.dma_start(out=out_dram[b, s], in_=results[unit][:])
 
-        load_w_head(0)
-        load_w_head(1)
-        load_w_head(2)
-        load_unit(0)
-        load_w_head(3)
-        load_unit(1)
+        loads = [(load_w_head, 0), (load_w_head, 1), (load_w_head, 2), (load_g, 0), (load_w_head, 3)]
+        for unit in range(LEAD):
+            loads.append((load_attn, unit, 0, HEADS))
+            loads.insert(len(loads) - 1, (load_g, unit + 1))
+            if 1 <= unit <= H - HEADS:
+                loads.append((load_w_head, HEADS + unit - 1))
+        loads.extend((load_attn, unit, HEADS, HEADS) for unit in range(LEAD))
+        loads.append((load_attn, LEAD, 0, H))
+        for unit in range(LEAD + 1, UNITS):
+            loads.extend([(load_g, unit), (load_attn, unit, 0, H)])
+
+        def ask(count):
+            for call in loads[:count]:
+                call[0](*call[1:])
+            loads[:] = loads[count:]
+
+        ask(FIRST_LOADS)
         for h in range(3):
             flip_w_head(h, nc.vector.tensor_copy if h == 1 else nc.scalar.copy)
         quantise_w_head(0)
@@ -197,11 +213,7 @@ def tile_localtemporalattention_pa_kernel(tc, attn, v, W_out, grad_out, out):
                 quantise_unit(0)
 
         for tick in range(STEPS + 3):
-            if HEADS + tick < H:
-                load_w_head(HEADS + tick)
-            for unit in range(2, UNITS):
-                if tick == max(unit - 2, FIRST[unit] - LOAD_AHEAD):
-                    load_unit(unit)
+            ask(LOADS_PER_TICK)
             w_head = HEADS + tick - 2
             if HEADS <= w_head < H:
                 flip_w_head(w_head, nc.scalar.copy)

@@ -23,12 +23,12 @@ HALVES = C // BANK
 HEADS = BANK // HD
 UNITS = B * S
 LEAD = 8
-ORDER = [(unit, half) for half in range(HALVES) for unit in range(LEAD)] + [
+STEPS = [(unit, half) for half in range(HALVES) for unit in range(LEAD)] + [
     (unit, half) for unit in range(LEAD, UNITS) for half in range(HALVES)
 ]
-STEPS = len(ORDER)
-FIRST = [ORDER.index((unit, 0)) for unit in range(UNITS)]
-FIRST_LOADS, LOADS_PER_TICK = 9, 3
+PAIR = 2
+PAIRS = len(STEPS) // PAIR
+FIRST_LOADS, LOADS_PER_TICK = 9, 6
 
 FLOPS = 2 * B * T * S * C * CO + 2 * B * H * S * T * T * HD
 BYTES = 2 * (B * H * S * T * T + C * CO + B * T * S * CO) + 4 * B * T * S * C
@@ -47,7 +47,7 @@ def tile_localtemporalattention_pa_kernel(tc, attn, v, W_out, grad_out, out):
         g_pool = ctx.enter_context(tc.tile_pool(name="g_rows", bufs=UNITS))
         attn_pool = ctx.enter_context(tc.tile_pool(name="attn_rows", bufs=UNITS))
         codes_pool = ctx.enter_context(tc.tile_pool(name="g_codes", bufs=UNITS))
-        stage = ctx.enter_context(tc.tile_pool(name="stage", bufs=5))
+        stage = ctx.enter_context(tc.tile_pool(name="stage", bufs=6))
         result_pool = ctx.enter_context(tc.tile_pool(name="result", bufs=LEAD + 2))
         psum = ctx.enter_context(tc.psum_pool(name="psum", bufs=8))
         ctx.enter_context(tc.manual_schedule())
@@ -122,13 +122,8 @@ def tile_localtemporalattention_pa_kernel(tc, attn, v, W_out, grad_out, out):
                 out=g_codes[unit][:].bitcast(E5M2_X4), scales=g_scales[unit][:], in_=g_grouped[unit][:]
             )
 
-        def is_split(step):
-            return sum(ORDER[step]) % 2 == 1
-
         def widen_step(step):
-            unit, half = ORDER[step]
-            if is_split(step):
-                return
+            unit, half = STEPS[step]
             attn_f32[step] = stage.tile([P, HEADS * T], F32, name="attn_f32")
             nc.vector.tensor_copy(
                 out=attn_f32[step][:],
@@ -136,7 +131,7 @@ def tile_localtemporalattention_pa_kernel(tc, attn, v, W_out, grad_out, out):
             )
 
         def project_step(step):
-            unit, half = ORDER[step]
+            unit, half = STEPS[step]
             acc = psum.tile([P, BANK], F32, tag="bank", name="acc")
             for c in range(PASSES):
                 first = c * C + half * BANK
@@ -149,7 +144,7 @@ def tile_localtemporalattention_pa_kernel(tc, attn, v, W_out, grad_out, out):
                     start=(c == 0),
                     stop=(c == PASSES - 1),
                 )
-            if is_split(step):
+            if step % PAIR == 1:
                 high = stage.tile([P, BANK], BF16, name="gctx_high")
                 nc.scalar.copy(out=high[:], in_=acc[:])
                 low = stage.tile([P, BANK], BF16, name="gctx_low")
@@ -160,10 +155,10 @@ def tile_localtemporalattention_pa_kernel(tc, attn, v, W_out, grad_out, out):
                 nc.scalar.copy(out=gctx[step][:], in_=acc[:])
 
         def mix_step(step):
-            unit, half = ORDER[step]
+            unit, half = STEPS[step]
             b, s = divmod(unit, S)
             mixed = psum.tile([P, BANK], F32, tag="bank", name="mixed")
-            if is_split(step):
+            if step % PAIR == 1:
                 weights, first, terms = attn_rows[unit], half * HEADS * T, gctx[step]
             else:
                 weights, first, terms = attn_f32[step], 0, (gctx[step],)
@@ -185,15 +180,17 @@ def tile_localtemporalattention_pa_kernel(tc, attn, v, W_out, grad_out, out):
             elif half == HALVES - 1:
                 nc.sync.dma_start(out=out_dram[b, s], in_=results[unit][:])
 
-        loads = [(load_w_head, 0), (load_w_head, 1), (load_w_head, 2), (load_g, 0), (load_w_head, 3)]
-        for unit in range(LEAD):
-            loads.append((load_attn, unit, 0, HEADS))
-            loads.insert(len(loads) - 1, (load_g, unit + 1))
-            if 1 <= unit <= H - HEADS:
-                loads.append((load_w_head, HEADS + unit - 1))
+        loads = [(load_w_head, h) for h in range(HEADS)]
+        loads.insert(HEADS - 1, (load_g, 0))
+        loads.extend((load_g, unit) for unit in range(1, 4))
+        for unit in range(0, LEAD, PAIR):
+            if HEADS + unit // PAIR < H:
+                loads.append((load_w_head, HEADS + unit // PAIR))
+            if unit + 2 * PAIR < LEAD:
+                loads.extend((load_g, unit + 2 * PAIR + i) for i in range(PAIR))
+            loads.extend((load_attn, unit + i, 0, HEADS) for i in range(PAIR))
         loads.extend((load_attn, unit, HEADS, HEADS) for unit in range(LEAD))
-        loads.append((load_attn, LEAD, 0, H))
-        for unit in range(LEAD + 1, UNITS):
+        for unit in range(LEAD, UNITS):
             loads.extend([(load_g, unit), (load_attn, unit, 0, H)])
 
         def ask(count):
@@ -201,31 +198,46 @@ def tile_localtemporalattention_pa_kernel(tc, attn, v, W_out, grad_out, out):
                 call[0](*call[1:])
             loads[:] = loads[count:]
 
+        def prepare(w_heads, units):
+            for h in w_heads:
+                flip_w_head(h, nc.scalar.copy)
+            for unit in units:
+                flip_unit(unit)
+            for h in w_heads:
+                quantise_w_head(h)
+            for unit in units:
+                quantise_unit(unit)
+
         ask(FIRST_LOADS)
         for h in range(3):
             flip_w_head(h, nc.vector.tensor_copy if h == 1 else nc.scalar.copy)
         quantise_w_head(0)
         flip_unit(0)
         flip_w_head(3, nc.scalar.copy)
-        for h in range(1, HEADS):
-            quantise_w_head(h)
-            if h == HEADS - 2:
-                quantise_unit(0)
+        flip_unit(1)
+        quantise_w_head(1)
+        quantise_w_head(2)
+        quantise_unit(0)
+        quantise_w_head(3)
+        quantise_unit(1)
 
-        for tick in range(STEPS + 3):
+        for tick in range(PAIRS + 1):
             ask(LOADS_PER_TICK)
-            w_head = HEADS + tick - 2
-            if HEADS <= w_head < H:
-                flip_w_head(w_head, nc.scalar.copy)
-            if 0 < tick and tick in FIRST:
-                flip_unit(FIRST.index(tick))
-            if HEADS <= w_head < H:
-                quantise_w_head(w_head)
-            if 0 <= tick - 1 < STEPS:
-                widen_step(tick - 1)
-            if 0 < tick and tick in FIRST:
-                quantise_unit(FIRST.index(tick))
-            if 0 <= tick - 1 < STEPS:
-                project_step(tick - 1)
-            if 0 <= tick - 3:
-                mix_step(tick - 3)
+            if tick == 1:
+                prepare([], [4, 5])
+            elif tick == 2:
+                prepare([5], [6, 7])
+            elif tick == 3:
+                prepare([6, 7], [])
+            elif LEAD - PAIR <= tick < UNITS - PAIR and tick % 2 == 0:
+                prepare([], [tick + 2, tick + 3])
+            if 0 < tick:
+                widen_step(PAIR * tick - 2)
+            if tick < PAIRS:
+                project_step(PAIR * tick)
+                project_step(PAIR * tick + 1)
+            if tick == 0:
+                prepare([4], [2, 3])
+            if 0 < tick:
+                mix_step(PAIR * tick - 2)
+                mix_step(PAIR * tick - 1)

@@ -112,8 +112,8 @@ def tile_localtemporalattention_pa_kernel(tc, attn, v, W_out, grad_out, out):
                     in_=w_grouped[h][:, c * HD * PACK : (c + 1) * HD * PACK],
                 )
 
-        def flip_unit(unit):
-            g_grouped[unit] = flip_rows(g_rows[unit], nc.vector.tensor_copy)
+        def flip_unit(unit, copy):
+            g_grouped[unit] = flip_rows(g_rows[unit], copy)
 
         def quantise_unit(unit):
             g_codes[unit] = codes_pool.tile([P, PASSES * T], U32, name="g_codes", align_bytes=64)
@@ -147,37 +147,46 @@ def tile_localtemporalattention_pa_kernel(tc, attn, v, W_out, grad_out, out):
             if step % PAIR == 1:
                 high = stage.tile([P, BANK], BF16, name="gctx_high")
                 nc.scalar.copy(out=high[:], in_=acc[:])
-                low = stage.tile([P, BANK], BF16, name="gctx_low")
-                nc.vector.tensor_sub(out=low[:], in0=acc[:], in1=high[:])
-                gctx[step] = (high, low)
+                gctx[step] = (high, acc)
             else:
                 gctx[step] = stage.tile([P, BANK], F32, name="gctx")
                 nc.scalar.copy(out=gctx[step][:], in_=acc[:])
 
+        def split_step(step):
+            high, acc = gctx[step]
+            low = stage.tile([P, BANK], BF16, name="gctx_low")
+            nc.vector.tensor_sub(out=low[:], in0=acc[:], in1=high[:])
+            gctx[step] = (high, low)
+
         def mix_step(step):
             unit, half = STEPS[step]
             b, s = divmod(unit, S)
-            mixed = psum.tile([P, BANK], F32, tag="bank", name="mixed")
             if step % PAIR == 1:
                 weights, first, terms = attn_rows[unit], half * HEADS * T, gctx[step]
             else:
                 weights, first, terms = attn_f32[step], 0, (gctx[step],)
-            for j in range(HEADS):
-                for i, term in enumerate(terms):
-                    nc.tensor.matmul(
-                        out=mixed[:, j * HD : (j + 1) * HD],
-                        lhsT=weights[:, first + j * T : first + (j + 1) * T],
-                        rhs=term[:, j * HD : (j + 1) * HD],
-                        start=(i == 0),
-                        stop=(i == len(terms) - 1),
-                    )
             if half == 0:
                 results[unit] = result_pool.tile([P, C], F32, name="result")
-            columns = slice(half * BANK, (half + 1) * BANK)
-            nc.scalar.copy(out=results[unit][:, columns], in_=mixed[:])
-            if unit == UNITS - 1:
-                nc.sync.dma_start(out=out_dram[b, s][:, columns], in_=results[unit][:, columns])
-            elif half == HALVES - 1:
+            parts = 2 if step == len(STEPS) - 1 else 1
+            width = BANK // parts
+            for part in range(parts):
+                mixed = psum.tile([P, BANK], F32, tag="bank", name="mixed")
+                for j in range(part * width // HD, (part + 1) * width // HD):
+                    for i, term in enumerate(terms):
+                        nc.tensor.matmul(
+                            out=mixed[:, j * HD : (j + 1) * HD],
+                            lhsT=weights[:, first + j * T : first + (j + 1) * T],
+                            rhs=term[:, j * HD : (j + 1) * HD],
+                            start=(i == 0),
+                            stop=(i == len(terms) - 1),
+                        )
+                here = slice(part * width, (part + 1) * width)
+                columns = slice(half * BANK + part * width, half * BANK + (part + 1) * width)
+                copy = nc.vector.tensor_copy if part else nc.scalar.copy
+                copy(out=results[unit][:, columns], in_=mixed[:, here])
+                if unit == UNITS - 1:
+                    nc.sync.dma_start(out=out_dram[b, s][:, columns], in_=results[unit][:, columns])
+            if half == HALVES - 1 and unit < UNITS - 1:
                 nc.sync.dma_start(out=out_dram[b, s], in_=results[unit][:])
 
         loads = [(load_w_head, h) for h in range(HEADS)]
@@ -198,46 +207,47 @@ def tile_localtemporalattention_pa_kernel(tc, attn, v, W_out, grad_out, out):
                 call[0](*call[1:])
             loads[:] = loads[count:]
 
-        def prepare(w_heads, units):
+        ask(FIRST_LOADS)
+        flip_w_head(0, nc.scalar.copy)
+        flip_w_head(1, nc.vector.tensor_copy)
+        flip_w_head(2, nc.scalar.copy)
+        quantise_w_head(0)
+        flip_unit(0, nc.vector.tensor_copy)
+        flip_w_head(3, nc.scalar.copy)
+        quantise_w_head(1)
+        quantise_w_head(2)
+        flip_unit(1, nc.scalar.copy)
+        quantise_unit(0)
+        quantise_w_head(3)
+        quantise_unit(1)
+        flip_unit(2, nc.vector.tensor_copy)
+        flip_unit(3, nc.vector.tensor_copy)
+        quantise_unit(2)
+        quantise_unit(3)
+
+        for tick in range(PAIRS + 1):
+            ask(LOADS_PER_TICK)
+            if 0 < tick < PAIRS:
+                widen_step(PAIR * tick)
+            if tick < PAIRS:
+                project_step(PAIR * tick)
+                project_step(PAIR * tick + 1)
+            w_heads = {0: [4], 1: [5], 2: [6, 7]}.get(tick, [])
+            units = []
+            if tick < 2 or LEAD - PAIR <= tick < UNITS - PAIR and tick % 2 == 0:
+                units = [tick + 2, tick + 3] if tick >= 2 else [2 * tick + 4, 2 * tick + 5]
             for h in w_heads:
                 flip_w_head(h, nc.scalar.copy)
             for unit in units:
-                flip_unit(unit)
+                flip_unit(unit, nc.vector.tensor_copy)
+            if tick < PAIRS:
+                split_step(PAIR * tick + 1)
             for h in w_heads:
                 quantise_w_head(h)
             for unit in units:
                 quantise_unit(unit)
-
-        ask(FIRST_LOADS)
-        for h in range(3):
-            flip_w_head(h, nc.vector.tensor_copy if h == 1 else nc.scalar.copy)
-        quantise_w_head(0)
-        flip_unit(0)
-        flip_w_head(3, nc.scalar.copy)
-        flip_unit(1)
-        quantise_w_head(1)
-        quantise_w_head(2)
-        quantise_unit(0)
-        quantise_w_head(3)
-        quantise_unit(1)
-
-        for tick in range(PAIRS + 1):
-            ask(LOADS_PER_TICK)
-            if tick == 1:
-                prepare([], [4, 5])
-            elif tick == 2:
-                prepare([5], [6, 7])
-            elif tick == 3:
-                prepare([6, 7], [])
-            elif LEAD - PAIR <= tick < UNITS - PAIR and tick % 2 == 0:
-                prepare([], [tick + 2, tick + 3])
-            if 0 < tick:
-                widen_step(PAIR * tick - 2)
-            if tick < PAIRS:
-                project_step(PAIR * tick)
-                project_step(PAIR * tick + 1)
             if tick == 0:
-                prepare([4], [2, 3])
+                widen_step(0)
             if 0 < tick:
                 mix_step(PAIR * tick - 2)
                 mix_step(PAIR * tick - 1)

@@ -28,7 +28,7 @@ STEPS = [(unit, half) for half in range(HALVES) for unit in range(LEAD)] + [
 ]
 PAIR = 2
 PAIRS = len(STEPS) // PAIR
-FIRST_LOADS, LOADS_PER_TICK = 9, 6
+FIRST_LOADS, LOADS_PER_TICK = 11, 6
 
 FLOPS = 2 * B * T * S * C * CO + 2 * B * H * S * T * T * HD
 BYTES = 2 * (B * H * S * T * T + C * CO + B * T * S * CO) + 4 * B * T * S * C
@@ -61,6 +61,7 @@ def tile_localtemporalattention_pa_kernel(tc, attn, v, W_out, grad_out, out):
         g_rows = {}
         attn_rows = {}
         w_grouped = {}
+        w_parts = {}
         g_grouped = {}
         g_codes = {}
         g_scales = {}
@@ -71,6 +72,12 @@ def tile_localtemporalattention_pa_kernel(tc, attn, v, W_out, grad_out, out):
         def load_w_head(h):
             w_rows[h] = w_pool.tile([P, CO], BF16, name="w_rows")
             nc.sync.dma_start(out=w_rows[h][:], in_=w_dram[h])
+
+        def load_w_part(h, c):
+            if c == 0:
+                w_rows[h] = w_pool.tile([P, CO], BF16, name="w_rows")
+            columns = slice(c * K_PASS, (c + 1) * K_PASS)
+            nc.sync.dma_start(out=w_rows[h][:, columns], in_=w_dram[h][:, columns])
 
         def load_g(unit):
             b, s = divmod(unit, S)
@@ -103,14 +110,30 @@ def tile_localtemporalattention_pa_kernel(tc, attn, v, W_out, grad_out, out):
         def flip_w_head(h, copy):
             w_grouped[h] = flip_rows(w_rows[h], copy)
 
+        def quantise_w(h, c, grouped):
+            first = c * C + h * HD
+            nc.vector.quantize_mx(
+                out=w_codes[:, first : first + HD].bitcast(E4M3_X4),
+                scales=w_scales[:, first : first + HD],
+                in_=grouped,
+            )
+
         def quantise_w_head(h):
             for c in range(PASSES):
-                first = c * C + h * HD
-                nc.vector.quantize_mx(
-                    out=w_codes[:, first : first + HD].bitcast(E4M3_X4),
-                    scales=w_scales[:, first : first + HD],
-                    in_=w_grouped[h][:, c * HD * PACK : (c + 1) * HD * PACK],
-                )
+                quantise_w(h, c, w_grouped[h][:, c * HD * PACK : (c + 1) * HD * PACK])
+
+        def flip_w_part(h, c, copy):
+            words = w_rows[h][:].bitcast(F32)
+            flipped = psum.tile([P, PLANES, P], F32, tag="bank", name="flipped_part")
+            for u in range(PLANES):
+                first = (PLANES * c + u) * P
+                nc.tensor.transpose(flipped[:, u, :], words[:, first : first + P], ident[:])
+            part = stage.tile([P, P * PACK], BF16, name="grouped_part", align_bytes=64)
+            copy(
+                out=part[:].bitcast(F32).rearrange("p (r u) -> p r u", u=PLANES),
+                in_=flipped[:].rearrange("p u r -> p r u"),
+            )
+            w_parts[c] = part
 
         def flip_unit(unit, copy):
             g_grouped[unit] = flip_rows(g_rows[unit], copy)
@@ -189,15 +212,14 @@ def tile_localtemporalattention_pa_kernel(tc, attn, v, W_out, grad_out, out):
             if half == HALVES - 1 and unit < UNITS - 1:
                 nc.sync.dma_start(out=out_dram[b, s], in_=results[unit][:])
 
-        loads = [(load_w_head, h) for h in range(HEADS)]
-        loads.insert(HEADS - 1, (load_g, 0))
-        loads.extend((load_g, unit) for unit in range(1, 4))
-        for unit in range(0, LEAD, PAIR):
-            if HEADS + unit // PAIR < H:
-                loads.append((load_w_head, HEADS + unit // PAIR))
-            if unit + 2 * PAIR < LEAD:
-                loads.extend((load_g, unit + 2 * PAIR + i) for i in range(PAIR))
-            loads.extend((load_attn, unit + i, 0, HEADS) for i in range(PAIR))
+        loads = [(load_w_head, 0), (load_w_head, 1), (load_w_head, 2), (load_g, 0)]
+        loads.extend((load_w_part, HEADS - 1, c) for c in range(PASSES))
+        loads.extend((load_g, unit) for unit in range(1, 6))
+        loads.extend((load_attn, unit, 0, HEADS) for unit in range(2))
+        loads.extend((load_g, unit) for unit in range(6, LEAD))
+        loads.extend((load_attn, unit, 0, HEADS) for unit in range(2, 4))
+        loads.extend((load_w_head, h) for h in range(HEADS, H))
+        loads.extend((load_attn, unit, 0, HEADS) for unit in range(4, LEAD))
         loads.extend((load_attn, unit, HEADS, HEADS) for unit in range(LEAD))
         for unit in range(LEAD, UNITS):
             loads.extend([(load_g, unit), (load_attn, unit, 0, H)])
@@ -211,16 +233,17 @@ def tile_localtemporalattention_pa_kernel(tc, attn, v, W_out, grad_out, out):
         flip_w_head(0, nc.scalar.copy)
         flip_w_head(1, nc.vector.tensor_copy)
         flip_w_head(2, nc.scalar.copy)
-        quantise_w_head(0)
-        flip_unit(0, nc.vector.tensor_copy)
-        flip_w_head(3, nc.scalar.copy)
-        quantise_w_head(1)
-        quantise_w_head(2)
-        flip_unit(1, nc.scalar.copy)
+        for h in range(HEADS - 1):
+            quantise_w_head(h)
+        flip_unit(0, nc.scalar.copy)
+        flip_w_part(HEADS - 1, 0, nc.scalar.copy)
+        flip_w_part(HEADS - 1, 1, nc.vector.tensor_copy)
         quantise_unit(0)
-        quantise_w_head(3)
-        quantise_unit(1)
+        for c in range(PASSES):
+            quantise_w(HEADS - 1, c, w_parts[c][:])
+        flip_unit(1, nc.scalar.copy)
         flip_unit(2, nc.vector.tensor_copy)
+        quantise_unit(1)
         flip_unit(3, nc.vector.tensor_copy)
         quantise_unit(2)
         quantise_unit(3)
@@ -232,22 +255,22 @@ def tile_localtemporalattention_pa_kernel(tc, attn, v, W_out, grad_out, out):
             if tick < PAIRS:
                 project_step(PAIR * tick)
                 project_step(PAIR * tick + 1)
-            w_heads = {0: [4], 1: [5], 2: [6, 7]}.get(tick, [])
+            w_heads = range(HEADS, H) if tick == 2 else []
             units = []
             if tick < 2 or LEAD - PAIR <= tick < UNITS - PAIR and tick % 2 == 0:
                 units = [tick + 2, tick + 3] if tick >= 2 else [2 * tick + 4, 2 * tick + 5]
             for h in w_heads:
-                flip_w_head(h, nc.scalar.copy)
+                flip_w_head(h, nc.vector.tensor_copy if h % 2 else nc.scalar.copy)
             for unit in units:
                 flip_unit(unit, nc.vector.tensor_copy)
+            if tick == 0:
+                widen_step(0)
             if tick < PAIRS:
                 split_step(PAIR * tick + 1)
             for h in w_heads:
                 quantise_w_head(h)
             for unit in units:
                 quantise_unit(unit)
-            if tick == 0:
-                widen_step(0)
             if 0 < tick:
                 mix_step(PAIR * tick - 2)
                 mix_step(PAIR * tick - 1)

@@ -30,6 +30,9 @@ PAIR = 2
 PAIRS = len(STEPS) // PAIR
 FIRST_LOADS, LOADS_PER_TICK = 11, 6
 
+HALF = P // 2
+REACH = 80
+
 FLOPS = 2 * B * T * S * C * CO + 2 * B * H * S * T * T * HD
 BYTES = 2 * (B * H * S * T * T + C * CO + B * T * S * CO) + 4 * B * T * S * C
 
@@ -45,7 +48,6 @@ def tile_localtemporalattention_pa_kernel(tc, attn, v, W_out, grad_out, out):
         const = ctx.enter_context(tc.tile_pool(name="const", bufs=1))
         w_pool = ctx.enter_context(tc.tile_pool(name="w_rows", bufs=H))
         g_pool = ctx.enter_context(tc.tile_pool(name="g_rows", bufs=UNITS))
-        attn_pool = ctx.enter_context(tc.tile_pool(name="attn_rows", bufs=UNITS))
         codes_pool = ctx.enter_context(tc.tile_pool(name="g_codes", bufs=UNITS))
         stage = ctx.enter_context(tc.tile_pool(name="stage", bufs=6))
         result_pool = ctx.enter_context(tc.tile_pool(name="result", bufs=LEAD + 2))
@@ -57,9 +59,16 @@ def tile_localtemporalattention_pa_kernel(tc, attn, v, W_out, grad_out, out):
         w_codes = const.tile([P, PASSES * C], U32, name="w_codes", align_bytes=64)
         w_scales = const.tile([P, PASSES * C], U8, name="w_scales", align_bytes=64)
 
+        attn_all = const.tile([P, UNITS * H * T], BF16, name="attn_all")
+        blocks = attn_all[:].rearrange("t (n u) -> t n u", u=T)
+
+        def clear_attn(first_unit, units):
+            here = slice(first_unit * H, (first_unit + units) * H)
+            nc.vector.memset(blocks[:HALF, here, REACH:].bitcast(F32), 0.0)
+            nc.vector.memset(blocks[HALF:, here, : T - REACH].bitcast(F32), 0.0)
+
         w_rows = {}
         g_rows = {}
-        attn_rows = {}
         w_grouped = {}
         w_parts = {}
         g_grouped = {}
@@ -86,12 +95,10 @@ def tile_localtemporalattention_pa_kernel(tc, attn, v, W_out, grad_out, out):
 
         def load_attn(unit, first, heads):
             b, s = divmod(unit, S)
-            if first == 0:
-                attn_rows[unit] = attn_pool.tile([P, H * T], BF16, name="attn_rows")
-            nc.sync.dma_start(
-                out=attn_rows[unit][:].rearrange("t (h u) -> t h u", h=H)[:, first : first + heads, :],
-                in_=attn_dram[b, s][:, first : first + heads, :],
-            )
+            here = slice(unit * H + first, unit * H + first + heads)
+            there = attn_dram[b, s][:, first : first + heads, :]
+            nc.sync.dma_start(out=blocks[:HALF, here, :REACH], in_=there[:HALF, :, :REACH])
+            nc.sync.dma_start(out=blocks[HALF:, here, T - REACH :], in_=there[HALF:, :, T - REACH :])
 
         def flip_rows(rows, copy):
             words = rows[:].bitcast(F32)
@@ -148,9 +155,9 @@ def tile_localtemporalattention_pa_kernel(tc, attn, v, W_out, grad_out, out):
         def widen_step(step):
             unit, half = STEPS[step]
             attn_f32[step] = stage.tile([P, HEADS * T], F32, name="attn_f32")
+            first = (unit * H + half * HEADS) * T
             nc.vector.tensor_copy(
-                out=attn_f32[step][:],
-                in_=attn_rows[unit][:, half * HEADS * T : (half + 1) * HEADS * T],
+                out=attn_f32[step][:], in_=attn_all[:, first : first + HEADS * T]
             )
 
         def project_step(step):
@@ -185,7 +192,7 @@ def tile_localtemporalattention_pa_kernel(tc, attn, v, W_out, grad_out, out):
             unit, half = STEPS[step]
             b, s = divmod(unit, S)
             if step % PAIR == 1:
-                weights, first, terms = attn_rows[unit], half * HEADS * T, gctx[step]
+                weights, first, terms = attn_all, (unit * H + half * HEADS) * T, gctx[step]
             else:
                 weights, first, terms = attn_f32[step], 0, (gctx[step],)
             if half == 0:
@@ -230,6 +237,7 @@ def tile_localtemporalattention_pa_kernel(tc, attn, v, W_out, grad_out, out):
             loads[:] = loads[count:]
 
         ask(FIRST_LOADS)
+        clear_attn(0, LEAD)
         flip_w_head(0, nc.scalar.copy)
         flip_w_head(1, nc.vector.tensor_copy)
         flip_w_head(2, nc.scalar.copy)
@@ -271,6 +279,8 @@ def tile_localtemporalattention_pa_kernel(tc, attn, v, W_out, grad_out, out):
                 quantise_w_head(h)
             for unit in units:
                 quantise_unit(unit)
+            if 3 <= tick < 3 + (UNITS - LEAD) // 2:
+                clear_attn(LEAD + 2 * (tick - 3), 2)
             if 0 < tick:
                 mix_step(PAIR * tick - 2)
                 mix_step(PAIR * tick - 1)

@@ -28,6 +28,10 @@ STEPS = [(unit, half) for half in range(HALVES) for unit in range(LEAD)] + [
 ]
 PAIR = 2
 PAIRS = len(STEPS) // PAIR
+STORED_BY_HALVES = 2
+
+SPLIT = [HEADS * (step % PAIR) for step in range(len(STEPS))]
+SPLIT[-PAIR] = 3
 FIRST_LOADS, LOADS_PER_TICK = 11, 6
 
 HALF = P // 2
@@ -75,7 +79,10 @@ def tile_localtemporalattention_pa_kernel(tc, attn, v, W_out, grad_out, out):
         g_codes = {}
         g_scales = {}
         attn_f32 = {}
+        sums = {}
         gctx = {}
+        high = {}
+        low = {}
         results = {}
 
         def load_w_head(h):
@@ -154,10 +161,11 @@ def tile_localtemporalattention_pa_kernel(tc, attn, v, W_out, grad_out, out):
 
         def widen_step(step):
             unit, half = STEPS[step]
+            first = (unit * H + half * HEADS + SPLIT[step]) * T
+            width = (HEADS - SPLIT[step]) * T
             attn_f32[step] = stage.tile([P, HEADS * T], F32, name="attn_f32")
-            first = (unit * H + half * HEADS) * T
             nc.vector.tensor_copy(
-                out=attn_f32[step][:], in_=attn_all[:, first : first + HEADS * T]
+                out=attn_f32[step][:, :width], in_=attn_all[:, first : first + width]
             )
 
         def project_step(step):
@@ -174,27 +182,25 @@ def tile_localtemporalattention_pa_kernel(tc, attn, v, W_out, grad_out, out):
                     start=(c == 0),
                     stop=(c == PASSES - 1),
                 )
-            if step % PAIR == 1:
-                high = stage.tile([P, BANK], BF16, name="gctx_high")
-                nc.scalar.copy(out=high[:], in_=acc[:])
-                gctx[step] = (high, acc)
-            else:
+            width = SPLIT[step] * HD
+            sums[step] = acc
+            if width:
+                high[step] = stage.tile([P, BANK], BF16, name="gctx_high")
+                nc.scalar.copy(out=high[step][:, :width], in_=acc[:, :width])
+            if width < BANK:
                 gctx[step] = stage.tile([P, BANK], F32, name="gctx")
-                nc.scalar.copy(out=gctx[step][:], in_=acc[:])
+                nc.scalar.copy(out=gctx[step][:, width:], in_=acc[:, width:])
 
         def split_step(step):
-            high, acc = gctx[step]
-            low = stage.tile([P, BANK], BF16, name="gctx_low")
-            nc.vector.tensor_sub(out=low[:], in0=acc[:], in1=high[:])
-            gctx[step] = (high, low)
+            width = SPLIT[step] * HD
+            low[step] = stage.tile([P, BANK], BF16, name="gctx_low")
+            nc.vector.tensor_sub(
+                out=low[step][:, :width], in0=sums[step][:, :width], in1=high[step][:, :width]
+            )
 
         def mix_step(step):
             unit, half = STEPS[step]
             b, s = divmod(unit, S)
-            if step % PAIR == 1:
-                weights, first, terms = attn_all, (unit * H + half * HEADS) * T, gctx[step]
-            else:
-                weights, first, terms = attn_f32[step], 0, (gctx[step],)
             if half == 0:
                 results[unit] = result_pool.tile([P, C], F32, name="result")
             parts = 2 if step == len(STEPS) - 1 else 1
@@ -202,10 +208,16 @@ def tile_localtemporalattention_pa_kernel(tc, attn, v, W_out, grad_out, out):
             for part in range(parts):
                 mixed = psum.tile([P, BANK], F32, tag="bank", name="mixed")
                 for j in range(part * width // HD, (part + 1) * width // HD):
+                    if j < SPLIT[step]:
+                        weights, first = attn_all, (unit * H + half * HEADS + j) * T
+                        terms = (high[step], low[step])
+                    else:
+                        weights, first = attn_f32[step], (j - SPLIT[step]) * T
+                        terms = (gctx[step],)
                     for i, term in enumerate(terms):
                         nc.tensor.matmul(
                             out=mixed[:, j * HD : (j + 1) * HD],
-                            lhsT=weights[:, first + j * T : first + (j + 1) * T],
+                            lhsT=weights[:, first : first + T],
                             rhs=term[:, j * HD : (j + 1) * HD],
                             start=(i == 0),
                             stop=(i == len(terms) - 1),
@@ -214,9 +226,9 @@ def tile_localtemporalattention_pa_kernel(tc, attn, v, W_out, grad_out, out):
                 columns = slice(half * BANK + part * width, half * BANK + (part + 1) * width)
                 copy = nc.vector.tensor_copy if part else nc.scalar.copy
                 copy(out=results[unit][:, columns], in_=mixed[:, here])
-                if unit == UNITS - 1:
+                if unit >= UNITS - STORED_BY_HALVES:
                     nc.sync.dma_start(out=out_dram[b, s][:, columns], in_=results[unit][:, columns])
-            if half == HALVES - 1 and unit < UNITS - 1:
+            if half == HALVES - 1 and unit < UNITS - STORED_BY_HALVES:
                 nc.sync.dma_start(out=out_dram[b, s], in_=results[unit][:])
 
         loads = [(load_w_head, 0), (load_w_head, 1), (load_w_head, 2), (load_g, 0)]
@@ -273,8 +285,9 @@ def tile_localtemporalattention_pa_kernel(tc, attn, v, W_out, grad_out, out):
                 flip_unit(unit, nc.vector.tensor_copy)
             if tick == 0:
                 widen_step(0)
-            if tick < PAIRS:
-                split_step(PAIR * tick + 1)
+            for step in range(PAIR * tick, min(PAIR * tick + PAIR, len(STEPS))):
+                if SPLIT[step]:
+                    split_step(step)
             for h in w_heads:
                 quantise_w_head(h)
             for unit in units:

from contextlib import ExitStack

import concourse.mybir as mybir
from concourse.masks import make_identity

F32 = mybir.dt.float32
BF16 = mybir.dt.bfloat16
U32 = mybir.dt.uint32
U8 = mybir.dt.uint8
E4M3_X4 = mybir.dt.float8_e4m3fn_x4
E5M2_X4 = mybir.dt.float8_e5m2_x4

P = 128
B, T, S, H, HD = 2, 128, 8, 8, 128
C = H * HD
CO = 1024
PACK = 4
K_PASS = P * PACK
PASSES = CO // K_PASS
PLANES = 2
BANK = 512
HALVES = C // BANK
HEADS = BANK // HD
UNITS = B * S
LEAD = 8
STEPS = [(unit, half) for half in range(HALVES) for unit in range(LEAD)] + [
    (unit, half) for unit in range(LEAD, UNITS) for half in range(HALVES)
]
PAIR = 2
PAIRS = len(STEPS) // PAIR
STORED_BY_HALVES = 2

SPLIT = [HEADS * (step % PAIR) for step in range(len(STEPS))]
SPLIT[-PAIR] = 3
FIRST_LOADS, LOADS_PER_TICK = 11, 6

HALF = P // 2
REACH = 80

FLOPS = 2 * B * T * S * C * CO + 2 * B * H * S * T * T * HD
BYTES = 2 * (B * H * S * T * T + C * CO + B * T * S * CO) + 4 * B * T * S * C


def tile_localtemporalattention_pa_kernel(tc, attn, v, W_out, grad_out, out):
    nc = tc.nc
    w_dram = W_out.rearrange("(h p) k -> h p k", p=P)
    g_dram = grad_out.rearrange("b (t s) k -> b s t k", s=S)
    attn_dram = attn.rearrange("b h s t u -> b s t h u")
    out_dram = out.rearrange("b u s h d -> b s u (h d)")

    with ExitStack() as ctx:
        const = ctx.enter_context(tc.tile_pool(name="const", bufs=1))
        w_pool = ctx.enter_context(tc.tile_pool(name="w_rows", bufs=H))
        g_pool = ctx.enter_context(tc.tile_pool(name="g_rows", bufs=UNITS))
        codes_pool = ctx.enter_context(tc.tile_pool(name="g_codes", bufs=UNITS))
        stage = ctx.enter_context(tc.tile_pool(name="stage", bufs=6))
        result_pool = ctx.enter_context(tc.tile_pool(name="result", bufs=LEAD + 2))
        psum = ctx.enter_context(tc.psum_pool(name="psum", bufs=8))
        ctx.enter_context(tc.manual_schedule())

        ident = const.tile([P, P], F32, name="ident")
        make_identity(nc, ident[:])
        w_codes = const.tile([P, PASSES * C], U32, name="w_codes", align_bytes=64)
        w_scales = const.tile([P, PASSES * C], U8, name="w_scales", align_bytes=64)

        attn_all = const.tile([P, UNITS * H * T], BF16, name="attn_all")
        blocks = attn_all[:].rearrange("t (n u) -> t n u", u=T)

        def clear_attn(first_unit, units):
            here = slice(first_unit * H, (first_unit + units) * H)
            nc.vector.memset(blocks[:HALF, here, REACH:].bitcast(F32), 0.0)
            nc.vector.memset(blocks[HALF:, here, : T - REACH].bitcast(F32), 0.0)

        w_rows = {}
        g_rows = {}
        w_grouped = {}
        w_parts = {}
        g_grouped = {}
        g_codes = {}
        g_scales = {}
        attn_f32 = {}
        sums = {}
        gctx = {}
        high = {}
        low = {}
        results = {}

        def load_w_head(h):
            w_rows[h] = w_pool.tile([P, CO], BF16, name="w_rows")
            nc.sync.dma_start(out=w_rows[h][:], in_=w_dram[h])

        def load_w_part(h, c):
            if c == 0:
                w_rows[h] = w_pool.tile([P, CO], BF16, name="w_rows")
            columns = slice(c * K_PASS, (c + 1) * K_PASS)
            nc.sync.dma_start(out=w_rows[h][:, columns], in_=w_dram[h][:, columns])

        def load_g(unit):
            b, s = divmod(unit, S)
            g_rows[unit] = g_pool.tile([P, CO], BF16, name="g_rows")
            nc.sync.dma_start(out=g_rows[unit][:], in_=g_dram[b, s])

        def load_attn(unit, first, heads):
            b, s = divmod(unit, S)
            here = slice(unit * H + first, unit * H + first + heads)
            there = attn_dram[b, s][:, first : first + heads, :]
            nc.sync.dma_start(out=blocks[:HALF, here, :REACH], in_=there[:HALF, :, :REACH])
            nc.sync.dma_start(out=blocks[HALF:, here, T - REACH :], in_=there[HALF:, :, T - REACH :])

        def flip_rows(rows, copy):
            words = rows[:].bitcast(F32)
            flipped = psum.tile([P, PASSES, PLANES, P], F32, tag="bank", name="flipped")
            for c in range(PASSES):
                for u in range(PLANES):
                    first = (PLANES * c + u) * P
                    nc.tensor.transpose(flipped[:, c, u, :], words[:, first : first + P], ident[:])
            grouped = stage.tile([P, PASSES * P * PACK], BF16, name="grouped", align_bytes=64)
            copy(
                out=grouped[:].bitcast(F32).rearrange("p (c r u) -> p c r u", c=PASSES, u=PLANES),
                in_=flipped[:].rearrange("p c u r -> p c r u"),
            )
            return grouped

        def flip_w_head(h, copy):
            w_grouped[h] = flip_rows(w_rows[h], copy)

        def quantise_w(h, c, grouped):
            first = c * C + h * HD
            nc.vector.quantize_mx(
                out=w_codes[:, first : first + HD].bitcast(E4M3_X4),
                scales=w_scales[:, first : first + HD],
                in_=grouped,
            )

        def quantise_w_head(h):
            for c in range(PASSES):
                quantise_w(h, c, w_grouped[h][:, c * HD * PACK : (c + 1) * HD * PACK])

        def flip_w_part(h, c, copy):
            words = w_rows[h][:].bitcast(F32)
            flipped = psum.tile([P, PLANES, P], F32, tag="bank", name="flipped_part")
            for u in range(PLANES):
                first = (PLANES * c + u) * P
                nc.tensor.transpose(flipped[:, u, :], words[:, first : first + P], ident[:])
            part = stage.tile([P, P * PACK], BF16, name="grouped_part", align_bytes=64)
            copy(
                out=part[:].bitcast(F32).rearrange("p (r u) -> p r u", u=PLANES),
                in_=flipped[:].rearrange("p u r -> p r u"),
            )
            w_parts[c] = part

        def flip_unit(unit, copy):
            g_grouped[unit] = flip_rows(g_rows[unit], copy)

        def quantise_unit(unit):
            g_codes[unit] = codes_pool.tile([P, PASSES * T], U32, name="g_codes", align_bytes=64)
            g_scales[unit] = codes_pool.tile([P, PASSES * T], U8, name="g_scales", align_bytes=64)
            nc.vector.quantize_mx(
                out=g_codes[unit][:].bitcast(E5M2_X4), scales=g_scales[unit][:], in_=g_grouped[unit][:]
            )

        def widen_step(step):
            unit, half = STEPS[step]
            first = (unit * H + half * HEADS + SPLIT[step]) * T
            width = (HEADS - SPLIT[step]) * T
            attn_f32[step] = stage.tile([P, HEADS * T], F32, name="attn_f32")
            nc.vector.tensor_copy(
                out=attn_f32[step][:, :width], in_=attn_all[:, first : first + width]
            )

        def project_step(step):
            unit, half = STEPS[step]
            acc = psum.tile([P, BANK], F32, tag="bank", name="acc")
            for c in range(PASSES):
                first = c * C + half * BANK
                nc.tensor.matmul_mx(
                    out=acc[:],
                    lhsT=g_codes[unit][:, c * T : (c + 1) * T].bitcast(E5M2_X4),
                    lhsT_scale=g_scales[unit][:, c * T : (c + 1) * T],
                    rhs=w_codes[:, first : first + BANK].bitcast(E4M3_X4),
                    rhs_scale=w_scales[:, first : first + BANK],
                    start=(c == 0),
                    stop=(c == PASSES - 1),
                )
            width = SPLIT[step] * HD
            sums[step] = acc
            if width:
                high[step] = stage.tile([P, BANK], BF16, name="gctx_high")
                nc.scalar.copy(out=high[step][:, :width], in_=acc[:, :width])
            if width < BANK:
                gctx[step] = stage.tile([P, BANK], F32, name="gctx")
                nc.scalar.copy(out=gctx[step][:, width:], in_=acc[:, width:])

        def split_step(step):
            width = SPLIT[step] * HD
            low[step] = stage.tile([P, BANK], BF16, name="gctx_low")
            nc.vector.tensor_sub(
                out=low[step][:, :width], in0=sums[step][:, :width], in1=high[step][:, :width]
            )

        def mix_step(step):
            unit, half = STEPS[step]
            b, s = divmod(unit, S)
            if half == 0:
                results[unit] = result_pool.tile([P, C], F32, name="result")
            parts = 2 if step == len(STEPS) - 1 else 1
            width = BANK // parts
            for part in range(parts):
                mixed = psum.tile([P, BANK], F32, tag="bank", name="mixed")
                for j in range(part * width // HD, (part + 1) * width // HD):
                    if j < SPLIT[step]:
                        weights, first = attn_all, (unit * H + half * HEADS + j) * T
                        terms = (high[step], low[step])
                    else:
                        weights, first = attn_f32[step], (j - SPLIT[step]) * T
                        terms = (gctx[step],)
                    for i, term in enumerate(terms):
                        nc.tensor.matmul(
                            out=mixed[:, j * HD : (j + 1) * HD],
                            lhsT=weights[:, first : first + T],
                            rhs=term[:, j * HD : (j + 1) * HD],
                            start=(i == 0),
                            stop=(i == len(terms) - 1),
                        )
                here = slice(part * width, (part + 1) * width)
                columns = slice(half * BANK + part * width, half * BANK + (part + 1) * width)
                copy = nc.vector.tensor_copy if part else nc.scalar.copy
                copy(out=results[unit][:, columns], in_=mixed[:, here])
                if unit >= UNITS - STORED_BY_HALVES:
                    nc.sync.dma_start(out=out_dram[b, s][:, columns], in_=results[unit][:, columns])
            if half == HALVES - 1 and unit < UNITS - STORED_BY_HALVES:
                nc.sync.dma_start(out=out_dram[b, s], in_=results[unit][:])

        loads = [(load_w_head, 0), (load_w_head, 1), (load_w_head, 2), (load_g, 0)]
        loads.extend((load_w_part, HEADS - 1, c) for c in range(PASSES))
        loads.extend((load_g, unit) for unit in range(1, 6))
        loads.extend((load_attn, unit, 0, HEADS) for unit in range(2))
        loads.extend((load_g, unit) for unit in range(6, LEAD))
        loads.extend((load_attn, unit, 0, HEADS) for unit in range(2, 4))
        loads.extend((load_w_head, h) for h in range(HEADS, H))
        loads.extend((load_attn, unit, 0, HEADS) for unit in range(4, LEAD))
        loads.extend((load_attn, unit, HEADS, HEADS) for unit in range(LEAD))
        for unit in range(LEAD, UNITS):
            loads.extend([(load_g, unit), (load_attn, unit, 0, H)])

        def ask(count):
            for call in loads[:count]:
                call[0](*call[1:])
            loads[:] = loads[count:]

        ask(FIRST_LOADS)
        clear_attn(0, LEAD)
        flip_w_head(0, nc.scalar.copy)
        flip_w_head(1, nc.vector.tensor_copy)
        flip_w_head(2, nc.scalar.copy)
        for h in range(HEADS - 1):
            quantise_w_head(h)
        flip_unit(0, nc.scalar.copy)
        flip_w_part(HEADS - 1, 0, nc.scalar.copy)
        flip_w_part(HEADS - 1, 1, nc.vector.tensor_copy)
        quantise_unit(0)
        for c in range(PASSES):
            quantise_w(HEADS - 1, c, w_parts[c][:])
        flip_unit(1, nc.scalar.copy)
        flip_unit(2, nc.vector.tensor_copy)
        quantise_unit(1)
        flip_unit(3, nc.vector.tensor_copy)
        quantise_unit(2)
        quantise_unit(3)

        for tick in range(PAIRS + 1):
            ask(LOADS_PER_TICK)
            if 0 < tick < PAIRS:
                widen_step(PAIR * tick)
            if tick < PAIRS:
                project_step(PAIR * tick)
                project_step(PAIR * tick + 1)
            w_heads = range(HEADS, H) if tick == 2 else []
            units = []
            if tick < 2 or LEAD - PAIR <= tick < UNITS - PAIR and tick % 2 == 0:
                units = [tick + 2, tick + 3] if tick >= 2 else [2 * tick + 4, 2 * tick + 5]
            for h in w_heads:
                flip_w_head(h, nc.vector.tensor_copy if h % 2 else nc.scalar.copy)
            for unit in units:
                flip_unit(unit, nc.vector.tensor_copy)
            if tick == 0:
                widen_step(0)
            for step in range(PAIR * tick, min(PAIR * tick + PAIR, len(STEPS))):
                if SPLIT[step]:
                    split_step(step)
            for h in w_heads:
                quantise_w_head(h)
            for unit in units:
                quantise_unit(unit)
            if 3 <= tick < 3 + (UNITS - LEAD) // 2:
                clear_attn(LEAD + 2 * (tick - 3), 2)
            if 0 < tick:
                mix_step(PAIR * tick - 2)
                mix_step(PAIR * tick - 1)
